import numpy as np
import ml_dtypes


def mxq(x, axis, fmt="e4m3"):
    dtype, down = {"e4m3": (ml_dtypes.float8_e4m3fn, 7), "e5m2": (ml_dtypes.float8_e5m2, 14)}[fmt]
    v = np.moveaxis(np.asarray(x, np.float32).astype(ml_dtypes.bfloat16).astype(np.float64), axis, -1)
    blocks = v.reshape(v.shape[:-1] + (-1, 32))
    amax = np.abs(blocks).max(-1, keepdims=True)
    byte = np.maximum(np.where(amax > 0, np.frexp(amax)[1] - 1 + 127, 0) - down, 1)
    scale = np.exp2(byte - 127.0)
    codes = (blocks / scale).astype(np.float32).astype(dtype).astype(np.float64)
    return np.moveaxis((codes * scale).reshape(v.shape), -1, axis)


WIDE = False


def mx_kscale(k):
    if not WIDE:
        return np.ones(k)
    levels = np.array([10, -10, 5, -5, 0])
    if k % 512:
        return np.exp2(np.random.permutation(np.resize(levels, k // 32))).repeat(32)
    a = np.empty((k // 512, 16))
    for p in range(k // 512):
        a[p, :8] = np.random.permutation(np.resize(levels, 8))
        for g in range(8):
            far = levels[np.abs(levels - a[p, g]) >= 10]
            a[p, g + 8] = far[np.random.randint(len(far))]
    return np.exp2(a.ravel()).repeat(32)


BF16 = ml_dtypes.bfloat16


def bf(x):
    return np.asarray(x, np.float32).astype(BF16)


def f64(x):
    return np.asarray(x).astype(np.float64)


B, T, DIM, H, D = 4, 1024, 512, 4, 128
E = H * D


def softmax(z):
    e = np.exp(z - z.max(-1, keepdims=True))
    return e / e.sum(-1, keepdims=True)


def setup_inputs():
    u = mx_kscale(E).reshape(H, D)
    q = softmax(3.0 * np.random.standard_normal((B, H, T, D)))
    k_sum = (T / D) * np.exp(0.3 * np.random.standard_normal((B, H, 1, D)))
    amp = 2.0 * np.sqrt(T * np.mean(q * q))
    context = k_sum.transpose(0, 1, 3, 2) * 0.2 * np.random.standard_normal((1, H, 1, D)) + amp * np.random.standard_normal((B, H, D, D))
    return {"q": bf(q * u[None, :, None, :]),
            "k_sum": bf(k_sum / u[None, :, None, :]),
            "context": bf(context * u[None, :, None, :] / u[None, :, :, None]),
            "Wp": bf(np.random.standard_normal((DIM, E)) * 2.0 / np.sqrt(E) / u.reshape(E)),
            "bp": bf(np.random.standard_normal(DIM) * 0.2)}


def reference(q, k_sum, context, Wp, bp):
    d_inv = 1.0 / (f64(q) * f64(k_sum)).sum(axis=-1, keepdims=True)
    o = (f64(q) @ f64(context)) * d_inv + f64(q)
    o = o.transpose(0, 2, 1, 3).reshape(B, T, E)
    return (mxq(o, 2, "e4m3") @ mxq(f64(Wp), 1, "e4m3").T) + f64(bp)

@@ -1,0 +1,219 @@
+from contextlib import ExitStack
+
+import concourse.mybir as mybir
+from concourse.masks import make_identity
+
+BF16 = mybir.dt.bfloat16
+F32 = mybir.dt.float32
+U32 = mybir.dt.uint32
+U8 = mybir.dt.uint8
+FP8X4 = mybir.dt.float8_e4m3fn_x4
+MULT = mybir.AluOpType.mult
+ADD = mybir.AluOpType.add
+
+P = 128
+B, H, T, D = 4, 4, 1024, 128
+E = H * D
+DIM = 512
+SLOTS = T // P
+HALF = SLOTS // 2
+G = 2
+UNITS = G * H
+ROUNDS_PER_BATCH = SLOTS // G
+ROUNDS = B * ROUNDS_PER_BATCH
+
+FLOPS = 2 * B * H * T * D * D + 2 * B * H * T * D + 2 * B * T * E * DIM
+
+
+def tile_linearattention_pb_kernel(tc, q, k_sum, context, Wp, bp, out):
+    nc = tc.nc
+    with ExitStack() as stack:
+        const = stack.enter_context(tc.tile_pool(name="const", bufs=1))
+        work = stack.enter_context(tc.tile_pool(name="work", bufs=2))
+        results = stack.enter_context(tc.tile_pool(name="results", bufs=4))
+        psum = stack.enter_context(tc.psum_pool(name="psum", bufs=1))
+        stack.enter_context(tc.manual_schedule())
+
+        ident = const.tile([P, P], BF16)
+        make_identity(nc, ident[:])
+
+        ksum_rows = const.tile([P, D], BF16)
+        nc.vector.memset(ksum_rows[:], 0.0)
+        nc.sync.dma_start(out=ksum_rows[0 : B * H, :], in_=k_sum.rearrange("b h o d -> (b h o) d"))
+
+        bias = const.tile([P, DIM], BF16)
+        nc.scalar.dma_start(out=bias[:], in_=bp.partition_broadcast(P))
+
+        q_nat = {}
+        ctx = const.tile([P, B * H, D], BF16)
+        w_nat = const.tile([P, DIM // P, E], BF16)
+        for b in range(B):
+            q_view = q[b].rearrange("h (p j) d -> p h j d", j=SLOTS)
+            for half in range(SLOTS // HALF):
+                q_nat[(b, half)] = const.tile([P, H, HALF, D], BF16, name="q_nat_%d_%d" % (b, half))
+                nc.sync.dma_start(
+                    out=q_nat[(b, half)][:], in_=q_view[:, :, half * HALF : (half + 1) * HALF, :]
+                )
+                if half == 0:
+                    nc.sync.dma_start(
+                        out=ctx[:, b * H : (b + 1) * H, :], in_=context[b].rearrange("h d e -> d h e")
+                    )
+                if b == 0 and half == 0:
+                    nc.sync.dma_start(out=w_nat[:], in_=Wp.rearrange("(c p) k -> p c k", p=P))
+
+        ksum_bank = psum.tile([P, UNITS, P], BF16, tag="q_bank")
+        nc.tensor.transpose(ksum_bank[:, 0, :], ksum_rows[:], ident[:])
+        ksum_cols = const.tile([P, B * H], BF16)
+        nc.vector.tensor_copy(out=ksum_cols[:], in_=ksum_bank[:, 0, 0 : B * H])
+
+        w_codes = const.tile([P, DIM], U32, align_bytes=64)
+        w_scales = const.tile([P, DIM], U8, align_bytes=64)
+
+        def quantise_weights():
+            w_grouped = const.tile([P, DIM, H], BF16, align_bytes=64)
+            blocks_per_bank = UNITS // H
+            copies = [nc.scalar.copy, nc.vector.tensor_copy]
+            for g in range(G):
+                first = g * blocks_per_bank
+                w_bank = psum.tile([P, blocks_per_bank, H, P], BF16, tag="out_bank_%d" % g, name="w_bank")
+                for c in range(blocks_per_bank):
+                    for h in range(H):
+                        nc.tensor.transpose(
+                            w_bank[:, c, h, :], w_nat[:, first + c, h::H], ident[:]
+                        )
+                copies[g](
+                    out=w_grouped[:, first * P : (first + blocks_per_bank) * P, :].rearrange(
+                        "p (c n) h -> p c n h", c=blocks_per_bank
+                    ),
+                    in_=w_bank[:].rearrange("p c h n -> p c n h"),
+                )
+            nc.vector.quantize_mx(
+                out=w_codes[:].bitcast(FP8X4),
+                scales=w_scales[:],
+                in_=w_grouped[:].rearrange("p n h -> p (n h)"),
+            )
+
+        live = {}
+
+        def queries(r, g, h):
+            b, pair = divmod(r, ROUNDS_PER_BATCH)
+            half, j = divmod(pair * G + g, HALF)
+            return q_nat[(b, half)][:, h, j, :]
+
+        def transpose_queries(r):
+            q_bank = psum.tile([P, UNITS, P], BF16, tag="q_bank")
+            for g in range(G):
+                for h in range(H):
+                    nc.tensor.transpose(q_bank[:, g * H + h, :], queries(r, g, h), ident[:])
+            q_t = work.tile([P, UNITS, P], BF16)
+            nc.scalar.copy(out=q_t[:], in_=q_bank[:])
+            live[("q_t", r)] = q_t
+
+        def multiply_context(r):
+            b = r // ROUNDS_PER_BATCH
+            q_t = live[("q_t", r)]
+            den_bank = psum.tile([P, UNITS], F32)
+            live[("den", r)] = den_bank
+            for g in range(G):
+                attn_bank = psum.tile([P, H, D], F32, bufs=3)
+                live[("attn", r, g)] = attn_bank
+                for h in range(H):
+                    u = g * H + h
+                    nc.tensor.matmul(
+                        attn_bank[:, h, :], lhsT=q_t[:, u, :], rhs=ctx[:, b * H + h, :], start=True, stop=True
+                    )
+                    nc.tensor.matmul(
+                        den_bank[:, u : u + 1],
+                        lhsT=q_t[:, u, :],
+                        rhs=ksum_cols[:, b * H + h : b * H + h + 1],
+                        start=True,
+                        stop=True,
+                    )
+
+        def normalise(r):
+            d_inv = work.tile([P, UNITS], F32)
+            nc.vector.reciprocal(out=d_inv[:], in_=live[("den", r)][:])
+            om = work.tile([P, G, E], BF16)
+            for g in range(G):
+                for h in range(H):
+                    u = g * H + h
+                    nc.vector.scalar_tensor_tensor(
+                        out=om[:, g, h * D : (h + 1) * D],
+                        in0=live[("attn", r, g)][:, h, :],
+                        scalar=d_inv[:, u : u + 1],
+                        in1=queries(r, g, h),
+                        op0=MULT,
+                        op1=ADD,
+                    )
+            live[("om", r)] = om
+
+        def transpose_outputs(r):
+            om = live[("om", r)]
+            o_bank = psum.tile([P, G, H, P], BF16, tag="o_bank")
+            for g in range(G):
+                for h in range(H):
+                    nc.tensor.transpose(o_bank[:, g, h, :], om[:, g, h::H], ident[:])
+            live[("o_bank", r)] = o_bank
+
+        def regroup_outputs(r):
+            o_bank = live[("o_bank", r)]
+            grouped = work.tile([P, G, P, H], BF16, align_bytes=64)
+            nc.scalar.copy(out=grouped[:], in_=o_bank[:].rearrange("p g h t -> p g t h"))
+            live[("grouped", r)] = grouped
+
+        def quantise(r):
+            codes = work.tile([P, G * P], U32, align_bytes=64)
+            scales = work.tile([P, G * P], U8, align_bytes=64)
+            nc.vector.quantize_mx(
+                out=codes[:].bitcast(FP8X4),
+                scales=scales[:],
+                in_=live[("grouped", r)][:].rearrange("p g t h -> p (g t h)"),
+            )
+            live[("codes", r)] = codes
+            live[("scales", r)] = scales
+
+        def project(r):
+            for g in range(G):
+                tokens = slice(g * P, (g + 1) * P)
+                out_bank = psum.tile([P, DIM], F32, tag="out_bank_%d" % g, name="out_bank")
+                nc.tensor.matmul_mx(
+                    out=out_bank[:],
+                    lhsT=live[("codes", r)][:, tokens].bitcast(FP8X4),
+                    lhsT_scale=live[("scales", r)][:, tokens],
+                    rhs=w_codes[:].bitcast(FP8X4),
+                    rhs_scale=w_scales[:],
+                    start=True,
+                    stop=True,
+                )
+                live[("out", r, g)] = out_bank
+
+        def add_bias_and_store(r):
+            b, pair = divmod(r, ROUNDS_PER_BATCH)
+            result = results.tile([P, G, DIM], F32)
+            for g in range(G):
+                nc.vector.tensor_tensor(out=result[:, g, :], in0=live[("out", r, g)][:], in1=bias[:], op=ADD)
+            out_view = out[b].rearrange("(p j) n -> p j n", j=SLOTS)
+            nc.sync.dma_start(out=out_view[:, pair * G : (pair + 1) * G, :], in_=result[:])
+
+        def active(r):
+            return 0 <= r < ROUNDS
+
+        for c in range(-2, ROUNDS + 2):
+            if active(c - 1):
+                regroup_outputs(c - 1)
+            if active(c - 2):
+                project(c - 2)
+            if active(c + 2):
+                transpose_queries(c + 2)
+            if active(c):
+                normalise(c)
+            if active(c + 1):
+                multiply_context(c + 1)
+            if active(c):
+                transpose_outputs(c)
+            if c == 0:
+                quantise_weights()
+            if active(c - 2):
+                add_bias_and_store(c - 2)
+            if active(c - 1):
+                quantise(c - 1)

@@ -15,6 +15,7 @@ P = 128
 B, H, T, D = 4, 4, 1024, 128
 E = H * D
 DIM = 512
+PACK = 4
 SLOTS = T // P
 HALF = SLOTS // 2
 G = 2
@@ -36,6 +37,8 @@ def tile_linearattention_pb_kernel(tc, q, k_sum, context, Wp, bp, out):
 
         ident = const.tile([P, P], BF16)
         make_identity(nc, ident[:])
+        ident_words = const.tile([P, P], F32)
+        make_identity(nc, ident_words[:])
 
         ksum_rows = const.tile([P, D], BF16)
         nc.vector.memset(ksum_rows[:], 0.0)
@@ -70,27 +73,27 @@ def tile_linearattention_pb_kernel(tc, q, k_sum, context, Wp, bp, out):
         w_scales = const.tile([P, DIM], U8, align_bytes=64)
 
         def quantise_weights():
-            w_grouped = const.tile([P, DIM, H], BF16, align_bytes=64)
-            blocks_per_bank = UNITS // H
+            w_grouped = const.tile([P, DIM, PACK], BF16, align_bytes=64)
+            w_words = w_grouped[:].bitcast(F32)
+            blocks_per_bank = DIM // P // G
             copies = [nc.scalar.copy, nc.vector.tensor_copy]
             for g in range(G):
                 first = g * blocks_per_bank
-                w_bank = psum.tile([P, blocks_per_bank, H, P], BF16, tag="out_bank_%d" % g, name="w_bank")
+                w_bank = psum.tile([P, blocks_per_bank, 2, P], F32, tag="out_bank_%d" % g, name="w_bank")
                 for c in range(blocks_per_bank):
-                    for h in range(H):
-                        nc.tensor.transpose(
-                            w_bank[:, c, h, :], w_nat[:, first + c, h::H], ident[:]
-                        )
+                    nat_words = w_nat[:, first + c, :].bitcast(F32)
+                    for u in range(2):
+                        nc.tensor.transpose(w_bank[:, c, u, :], nat_words[:, u::2], ident_words[:])
                 copies[g](
-                    out=w_grouped[:, first * P : (first + blocks_per_bank) * P, :].rearrange(
-                        "p (c n) h -> p c n h", c=blocks_per_bank
+                    out=w_words[:, first * P : (first + blocks_per_bank) * P, :].rearrange(
+                        "p (c n) u -> p c n u", c=blocks_per_bank
                     ),
-                    in_=w_bank[:].rearrange("p c h n -> p c n h"),
+                    in_=w_bank[:].rearrange("p c u n -> p c n u"),
                 )
             nc.vector.quantize_mx(
                 out=w_codes[:].bitcast(FP8X4),
                 scales=w_scales[:],
-                in_=w_grouped[:].rearrange("p n h -> p (n h)"),
+                in_=w_grouped[:].rearrange("p n k -> p (n k)"),
             )
 
         live = {}
@@ -130,9 +133,13 @@ def tile_linearattention_pb_kernel(tc, q, k_sum, context, Wp, bp, out):
                         stop=True,
                     )
 
-        def normalise(r):
+        def invert(r):
             d_inv = work.tile([P, UNITS], F32)
             nc.vector.reciprocal(out=d_inv[:], in_=live[("den", r)][:])
+            live[("d_inv", r)] = d_inv
+
+        def normalise(r):
+            d_inv = live[("d_inv", r)]
             om = work.tile([P, G, E], BF16)
             for g in range(G):
                 for h in range(H):
@@ -149,16 +156,17 @@ def tile_linearattention_pb_kernel(tc, q, k_sum, context, Wp, bp, out):
 
         def transpose_outputs(r):
             om = live[("om", r)]
-            o_bank = psum.tile([P, G, H, P], BF16, tag="o_bank")
+            o_bank = psum.tile([P, G, 2, P], F32, tag="o_bank")
             for g in range(G):
-                for h in range(H):
-                    nc.tensor.transpose(o_bank[:, g, h, :], om[:, g, h::H], ident[:])
+                words = om[:, g, :].bitcast(F32)
+                for u in range(2):
+                    nc.tensor.transpose(o_bank[:, g, u, :], words[:, u::2], ident_words[:])
             live[("o_bank", r)] = o_bank
 
         def regroup_outputs(r):
             o_bank = live[("o_bank", r)]
-            grouped = work.tile([P, G, P, H], BF16, align_bytes=64)
-            nc.scalar.copy(out=grouped[:], in_=o_bank[:].rearrange("p g h t -> p g t h"))
+            grouped = work.tile([P, G, P, PACK], BF16, align_bytes=64)
+            nc.scalar.copy(out=grouped[:].bitcast(F32), in_=o_bank[:].rearrange("p g u t -> p g t u"))
             live[("grouped", r)] = grouped
 
         def quantise(r):
@@ -167,7 +175,7 @@ def tile_linearattention_pb_kernel(tc, q, k_sum, context, Wp, bp, out):
             nc.vector.quantize_mx(
                 out=codes[:].bitcast(FP8X4),
                 scales=scales[:],
-                in_=live[("grouped", r)][:].rearrange("p g t h -> p (g t h)"),
+                in_=live[("grouped", r)][:].rearrange("p g t k -> p (g t k)"),
             )
             live[("codes", r)] = codes
             live[("scales", r)] = scales
@@ -199,21 +207,20 @@ def tile_linearattention_pb_kernel(tc, q, k_sum, context, Wp, bp, out):
             return 0 <= r < ROUNDS
 
         for c in range(-2, ROUNDS + 2):
-            if active(c - 1):
-                regroup_outputs(c - 1)
-            if active(c - 2):
-                project(c - 2)
             if active(c + 2):
                 transpose_queries(c + 2)
+            if active(c - 1):
+                transpose_outputs(c - 1)
+                regroup_outputs(c - 1)
+            if active(c - 2):
+                quantise(c - 2)
+                project(c - 2)
             if active(c):
                 normalise(c)
-            if active(c + 1):
-                multiply_context(c + 1)
-            if active(c):
-                transpose_outputs(c)
-            if c == 0:
-                quantise_weights()
             if active(c - 2):
                 add_bias_and_store(c - 2)
-            if active(c - 1):
-                quantise(c - 1)
+            if active(c + 1):
+                multiply_context(c + 1)
+                invert(c + 1)
+            if c == 0:
+                quantise_weights()

@@ -17,11 +17,11 @@ E = H * D
 DIM = 512
 PACK = 4
 SLOTS = T // P
-HALF = SLOTS // 2
 G = 2
 UNITS = G * H
 ROUNDS_PER_BATCH = SLOTS // G
 ROUNDS = B * ROUNDS_PER_BATCH
+RELIEF = 2
 
 FLOPS = 2 * B * H * T * D * D + 2 * B * H * T * D + 2 * B * T * E * DIM
 
@@ -42,32 +42,39 @@ def tile_linearattention_pb_kernel(tc, q, k_sum, context, Wp, bp, out):
 
         ksum_rows = const.tile([P, D], BF16)
         nc.vector.memset(ksum_rows[:], 0.0)
-        nc.sync.dma_start(out=ksum_rows[0 : B * H, :], in_=k_sum.rearrange("b h o d -> (b h o) d"))
-
-        bias = const.tile([P, DIM], BF16)
-        nc.scalar.dma_start(out=bias[:], in_=bp.partition_broadcast(P))
 
         q_nat = {}
         ctx = const.tile([P, B * H, D], BF16)
         w_nat = const.tile([P, DIM // P, E], BF16)
-        for b in range(B):
-            q_view = q[b].rearrange("h (p j) d -> p h j d", j=SLOTS)
-            for half in range(SLOTS // HALF):
-                q_nat[(b, half)] = const.tile([P, H, HALF, D], BF16, name="q_nat_%d_%d" % (b, half))
-                nc.sync.dma_start(
-                    out=q_nat[(b, half)][:], in_=q_view[:, :, half * HALF : (half + 1) * HALF, :]
-                )
-                if half == 0:
-                    nc.sync.dma_start(
-                        out=ctx[:, b * H : (b + 1) * H, :], in_=context[b].rearrange("h d e -> d h e")
-                    )
-                if b == 0 and half == 0:
-                    nc.sync.dma_start(out=w_nat[:], in_=Wp.rearrange("(c p) k -> p c k", p=P))
+        bias = const.tile([P, DIM], BF16)
 
-        ksum_bank = psum.tile([P, UNITS, P], BF16, tag="q_bank")
-        nc.tensor.transpose(ksum_bank[:, 0, :], ksum_rows[:], ident[:])
+        def load_queries(b, first, width):
+            chunk = const.tile([P, H, width, D], BF16, name="q_nat_%d_%d" % (b, first))
+            q_view = q[b].rearrange("h (p j) d -> p h j d", j=SLOTS)
+            nc.sync.dma_start(out=chunk[:], in_=q_view[:, :, first : first + width, :])
+            for j in range(width):
+                q_nat[(b, first + j)] = (chunk, j)
+
+        def load_context(b):
+            nc.sync.dma_start(out=ctx[:, b * H : (b + 1) * H, :], in_=context[b].rearrange("h d e -> d h e"))
+
+        load_queries(0, 0, G)
+        nc.sync.dma_start(out=ksum_rows[0 : B * H, :], in_=k_sum.rearrange("b h o d -> (b h o) d"))
+        load_context(0)
+        load_queries(0, G, G)
+        nc.sync.dma_start(out=w_nat[:], in_=Wp.rearrange("(c p) k -> p c k", p=P))
+        load_queries(0, 2 * G, SLOTS - 2 * G)
+        nc.sync.dma_start(out=bias[:], in_=bp.partition_broadcast(P))
+        for b in range(1, B):
+            load_queries(b, 0, SLOTS)
+            load_context(b)
+
         ksum_cols = const.tile([P, B * H], BF16)
-        nc.vector.tensor_copy(out=ksum_cols[:], in_=ksum_bank[:, 0, 0 : B * H])
+
+        def transpose_ksum():
+            ksum_bank = psum.tile([P, P], BF16, tag="o_bank")
+            nc.tensor.transpose(ksum_bank[:], ksum_rows[:], ident[:])
+            nc.vector.tensor_copy(out=ksum_cols[:], in_=ksum_bank[:, 0 : B * H])
 
         w_codes = const.tile([P, DIM], U32, align_bytes=64)
         w_scales = const.tile([P, DIM], U8, align_bytes=64)
@@ -100,16 +107,20 @@ def tile_linearattention_pb_kernel(tc, q, k_sum, context, Wp, bp, out):
 
         def queries(r, g, h):
             b, pair = divmod(r, ROUNDS_PER_BATCH)
-            half, j = divmod(pair * G + g, HALF)
-            return q_nat[(b, half)][:, h, j, :]
+            chunk, j = q_nat[(b, pair * G + g)]
+            return chunk[:, h, j, :]
 
         def transpose_queries(r):
-            q_bank = psum.tile([P, UNITS, P], BF16, tag="q_bank")
-            for g in range(G):
-                for h in range(H):
-                    nc.tensor.transpose(q_bank[:, g * H + h, :], queries(r, g, h), ident[:])
             q_t = work.tile([P, UNITS, P], BF16)
-            nc.scalar.copy(out=q_t[:], in_=q_bank[:])
+            early_banks = {0: ["out_bank_0", "out_bank_1"], 1: ["q_bank", "o_bank"]}
+            banks = early_banks.get(r, ["q_bank"])
+            tiles = G // len(banks)
+            for i in range(len(banks)):
+                q_bank = psum.tile([P, tiles * H, P], BF16, tag=banks[i], name="q_bank")
+                for g in range(tiles):
+                    for h in range(H):
+                        nc.tensor.transpose(q_bank[:, g * H + h, :], queries(r, i * tiles + g, h), ident[:])
+                nc.scalar.copy(out=q_t[:, i * tiles * H : (i + 1) * tiles * H, :], in_=q_bank[:])
             live[("q_t", r)] = q_t
 
         def multiply_context(r):
@@ -199,15 +210,27 @@ def tile_linearattention_pb_kernel(tc, q, k_sum, context, Wp, bp, out):
             b, pair = divmod(r, ROUNDS_PER_BATCH)
             result = results.tile([P, G, DIM], F32)
             for g in range(G):
-                nc.vector.tensor_tensor(out=result[:, g, :], in0=live[("out", r, g)][:], in1=bias[:], op=ADD)
+                if g == 1 and r % RELIEF == 0 and r < ROUNDS - RELIEF:
+                    plain = results.tile([P, DIM], F32)
+                    nc.scalar.copy(out=plain[:], in_=live[("out", r, g)][:])
+                    nc.gpsimd.tensor_tensor(out=result[:, g, :], in0=plain[:], in1=bias[:], op=ADD)
+                else:
+                    nc.vector.tensor_tensor(out=result[:, g, :], in0=live[("out", r, g)][:], in1=bias[:], op=ADD)
             out_view = out[b].rearrange("(p j) n -> p j n", j=SLOTS)
             nc.sync.dma_start(out=out_view[:, pair * G : (pair + 1) * G, :], in_=result[:])
 
         def active(r):
             return 0 <= r < ROUNDS
 
-        for c in range(-2, ROUNDS + 2):
-            if active(c + 2):
+        transpose_queries(0)
+        transpose_ksum()
+        multiply_context(0)
+        invert(0)
+        transpose_queries(1)
+        multiply_context(1)
+        transpose_queries(2)
+        for c in range(ROUNDS + 2):
+            if c > 0 and active(c + 2):
                 transpose_queries(c + 2)
             if active(c - 1):
                 transpose_outputs(c - 1)
@@ -219,8 +242,9 @@ def tile_linearattention_pb_kernel(tc, q, k_sum, context, Wp, bp, out):
                 normalise(c)
             if active(c - 2):
                 add_bias_and_store(c - 2)
-            if active(c + 1):
+            if c > 0 and active(c + 1):
                 multiply_context(c + 1)
+            if active(c + 1):
                 invert(c + 1)
             if c == 0:
                 quantise_weights()

@@ -21,7 +21,7 @@ G = 2
 UNITS = G * H
 ROUNDS_PER_BATCH = SLOTS // G
 ROUNDS = B * ROUNDS_PER_BATCH
-RELIEF = 2
+RELIEF = 1
 
 FLOPS = 2 * B * H * T * D * D + 2 * B * H * T * D + 2 * B * T * E * DIM
 
@@ -151,27 +151,30 @@ def tile_linearattention_pb_kernel(tc, q, k_sum, context, Wp, bp, out):
 
         def normalise(r):
             d_inv = live[("d_inv", r)]
-            om = work.tile([P, G, E], BF16)
+            om = work.tile([P, G, 2, H, D // PACK, 2], BF16)
             for g in range(G):
                 for h in range(H):
-                    u = g * H + h
-                    nc.vector.scalar_tensor_tensor(
-                        out=om[:, g, h * D : (h + 1) * D],
-                        in0=live[("attn", r, g)][:, h, :],
-                        scalar=d_inv[:, u : u + 1],
-                        in1=queries(r, g, h),
-                        op0=MULT,
-                        op1=ADD,
-                    )
+                    attn = live[("attn", r, g)][:, h, :].rearrange("p (a u i) -> p u a i", u=2, i=2)
+                    q_pairs = queries(r, g, h).rearrange("p (a u i) -> p u a i", u=2, i=2)
+                    unit = g * H + h
+                    for u in range(2):
+                        nc.vector.scalar_tensor_tensor(
+                            out=om[:, g, u, h, :, :],
+                            in0=attn[:, u, :, :],
+                            scalar=d_inv[:, unit : unit + 1],
+                            in1=q_pairs[:, u, :, :],
+                            op0=MULT,
+                            op1=ADD,
+                        )
             live[("om", r)] = om
 
         def transpose_outputs(r):
             om = live[("om", r)]
             o_bank = psum.tile([P, G, 2, P], F32, tag="o_bank")
             for g in range(G):
-                words = om[:, g, :].bitcast(F32)
                 for u in range(2):
-                    nc.tensor.transpose(o_bank[:, g, u, :], words[:, u::2], ident_words[:])
+                    words = om[:, g, u].rearrange("p h a i -> p (h a i)").bitcast(F32)
+                    nc.tensor.transpose(o_bank[:, g, u, :], words, ident_words[:])
             live[("o_bank", r)] = o_bank
 
         def regroup_outputs(r):
@@ -210,7 +213,7 @@ def tile_linearattention_pb_kernel(tc, q, k_sum, context, Wp, bp, out):
             b, pair = divmod(r, ROUNDS_PER_BATCH)
             result = results.tile([P, G, DIM], F32)
             for g in range(G):
-                if g == 1 and r % RELIEF == 0 and r < ROUNDS - RELIEF:
+                if g == 1 and r % RELIEF == 0 and r < ROUNDS - 2:
                     plain = results.tile([P, DIM], F32)
                     nc.scalar.copy(out=plain[:], in_=live[("out", r, g)][:])
                     nc.gpsimd.tensor_tensor(out=result[:, g, :], in0=plain[:], in1=bias[:], op=ADD)

@@ -19,6 +19,8 @@ PACK = 4
 SLOTS = T // P
 G = 2
 UNITS = G * H
+BANK_UNITS = 3
+CTX_PAD = 8
 ROUNDS_PER_BATCH = SLOTS // G
 ROUNDS = B * ROUNDS_PER_BATCH
 RELIEF = 1
@@ -44,7 +46,7 @@ def tile_linearattention_pb_kernel(tc, q, k_sum, context, Wp, bp, out):
         nc.vector.memset(ksum_rows[:], 0.0)
 
         q_nat = {}
-        ctx = const.tile([P, B * H, D], BF16)
+        ctx = const.tile([P, B * H, D + CTX_PAD], BF16)
         w_nat = const.tile([P, DIM // P, E], BF16)
         bias = const.tile([P, DIM], BF16)
 
@@ -56,7 +58,7 @@ def tile_linearattention_pb_kernel(tc, q, k_sum, context, Wp, bp, out):
                 q_nat[(b, first + j)] = (chunk, j)
 
         def load_context(b):
-            nc.sync.dma_start(out=ctx[:, b * H : (b + 1) * H, :], in_=context[b].rearrange("h d e -> d h e"))
+            nc.sync.dma_start(out=ctx[:, b * H : (b + 1) * H, 0:D], in_=context[b].rearrange("h d e -> d h e"))
 
         load_queries(0, 0, G)
         nc.sync.dma_start(out=ksum_rows[0 : B * H, :], in_=k_sum.rearrange("b h o d -> (b h o) d"))
@@ -69,12 +71,10 @@ def tile_linearattention_pb_kernel(tc, q, k_sum, context, Wp, bp, out):
             load_queries(b, 0, SLOTS)
             load_context(b)
 
-        ksum_cols = const.tile([P, B * H], BF16)
-
         def transpose_ksum():
             ksum_bank = psum.tile([P, P], BF16, tag="o_bank")
             nc.tensor.transpose(ksum_bank[:], ksum_rows[:], ident[:])
-            nc.vector.tensor_copy(out=ksum_cols[:], in_=ksum_bank[:, 0 : B * H])
+            nc.vector.tensor_copy(out=ctx[:, :, D], in_=ksum_bank[:, 0 : B * H])
 
         w_codes = const.tile([P, DIM], U32, align_bytes=64)
         w_scales = const.tile([P, DIM], U8, align_bytes=64)
@@ -126,27 +126,25 @@ def tile_linearattention_pb_kernel(tc, q, k_sum, context, Wp, bp, out):
         def multiply_context(r):
             b = r // ROUNDS_PER_BATCH
             q_t = live[("q_t", r)]
-            den_bank = psum.tile([P, UNITS], F32)
-            live[("den", r)] = den_bank
-            for g in range(G):
-                attn_bank = psum.tile([P, H, D], F32, bufs=3)
-                live[("attn", r, g)] = attn_bank
-                for h in range(H):
-                    u = g * H + h
+            for first in range(0, UNITS, BANK_UNITS):
+                units = range(first, min(first + BANK_UNITS, UNITS))
+                attn_bank = psum.tile([P, BANK_UNITS, D + 1], F32, bufs=4)
+                for u in units:
                     nc.tensor.matmul(
-                        attn_bank[:, h, :], lhsT=q_t[:, u, :], rhs=ctx[:, b * H + h, :], start=True, stop=True
-                    )
-                    nc.tensor.matmul(
-                        den_bank[:, u : u + 1],
+                        attn_bank[:, u - first, :],
                         lhsT=q_t[:, u, :],
-                        rhs=ksum_cols[:, b * H + h : b * H + h + 1],
+                        rhs=ctx[:, b * H + u % H, 0 : D + 1],
                         start=True,
                         stop=True,
                     )
+                    live[("attn", r, u)] = attn_bank[:, u - first, 0:D]
+                live[("den", r, first)] = attn_bank[:, 0 : len(units), D]
 
         def invert(r):
             d_inv = work.tile([P, UNITS], F32)
-            nc.vector.reciprocal(out=d_inv[:], in_=live[("den", r)][:])
+            for first in range(0, UNITS, BANK_UNITS):
+                den = live[("den", r, first)]
+                nc.vector.reciprocal(out=d_inv[:, first : min(first + BANK_UNITS, UNITS)], in_=den)
             live[("d_inv", r)] = d_inv
 
         def normalise(r):
@@ -154,9 +152,9 @@ def tile_linearattention_pb_kernel(tc, q, k_sum, context, Wp, bp, out):
             om = work.tile([P, G, 2, H, D // PACK, 2], BF16)
             for g in range(G):
                 for h in range(H):
-                    attn = live[("attn", r, g)][:, h, :].rearrange("p (a u i) -> p u a i", u=2, i=2)
                     q_pairs = queries(r, g, h).rearrange("p (a u i) -> p u a i", u=2, i=2)
                     unit = g * H + h
+                    attn = live[("attn", r, unit)].rearrange("p (a u i) -> p u a i", u=2, i=2)
                     for u in range(2):
                         nc.vector.scalar_tensor_tensor(
                             out=om[:, g, u, h, :, :],

@@ -23,7 +23,6 @@ BANK_UNITS = 3
 CTX_PAD = 8
 ROUNDS_PER_BATCH = SLOTS // G
 ROUNDS = B * ROUNDS_PER_BATCH
-RELIEF = 1
 
 FLOPS = 2 * B * H * T * D * D + 2 * B * H * T * D + 2 * B * T * E * DIM
 
@@ -79,11 +78,11 @@ def tile_linearattention_pb_kernel(tc, q, k_sum, context, Wp, bp, out):
         w_codes = const.tile([P, DIM], U32, align_bytes=64)
         w_scales = const.tile([P, DIM], U8, align_bytes=64)
 
-        def quantise_weights():
-            w_grouped = const.tile([P, DIM, PACK], BF16, align_bytes=64)
+        w_grouped = const.tile([P, DIM, PACK], BF16, align_bytes=64)
+
+        def transpose_weights():
             w_words = w_grouped[:].bitcast(F32)
             blocks_per_bank = DIM // P // G
-            copies = [nc.scalar.copy, nc.vector.tensor_copy]
             for g in range(G):
                 first = g * blocks_per_bank
                 w_bank = psum.tile([P, blocks_per_bank, 2, P], F32, tag="out_bank_%d" % g, name="w_bank")
@@ -91,12 +90,14 @@ def tile_linearattention_pb_kernel(tc, q, k_sum, context, Wp, bp, out):
                     nat_words = w_nat[:, first + c, :].bitcast(F32)
                     for u in range(2):
                         nc.tensor.transpose(w_bank[:, c, u, :], nat_words[:, u::2], ident_words[:])
-                copies[g](
+                nc.scalar.copy(
                     out=w_words[:, first * P : (first + blocks_per_bank) * P, :].rearrange(
                         "p (c n) u -> p c n u", c=blocks_per_bank
                     ),
                     in_=w_bank[:].rearrange("p c u n -> p c n u"),
                 )
+
+        def quantise_weights():
             nc.vector.quantize_mx(
                 out=w_codes[:].bitcast(FP8X4),
                 scales=w_scales[:],
@@ -211,7 +212,7 @@ def tile_linearattention_pb_kernel(tc, q, k_sum, context, Wp, bp, out):
             b, pair = divmod(r, ROUNDS_PER_BATCH)
             result = results.tile([P, G, DIM], F32)
             for g in range(G):
-                if g == 1 and r % RELIEF == 0 and r < ROUNDS - 2:
+                if (g == 1 or r % 2 == 1) and r < ROUNDS - 2:
                     plain = results.tile([P, DIM], F32)
                     nc.scalar.copy(out=plain[:], in_=live[("out", r, g)][:])
                     nc.gpsimd.tensor_tensor(out=result[:, g, :], in0=plain[:], in1=bias[:], op=ADD)
@@ -229,10 +230,11 @@ def tile_linearattention_pb_kernel(tc, q, k_sum, context, Wp, bp, out):
         invert(0)
         transpose_queries(1)
         multiply_context(1)
-        transpose_queries(2)
         for c in range(ROUNDS + 2):
-            if c > 0 and active(c + 2):
-                transpose_queries(c + 2)
+            if c > 0 and active(c + 1):
+                transpose_queries(c + 1)
+            if c == 1:
+                transpose_weights()
             if active(c - 1):
                 transpose_outputs(c - 1)
                 regroup_outputs(c - 1)
@@ -241,11 +243,11 @@ def tile_linearattention_pb_kernel(tc, q, k_sum, context, Wp, bp, out):
                 project(c - 2)
             if active(c):
                 normalise(c)
+            if c == 1:
+                quantise_weights()
             if active(c - 2):
                 add_bias_and_store(c - 2)
             if c > 0 and active(c + 1):
                 multiply_context(c + 1)
             if active(c + 1):
                 invert(c + 1)
-            if c == 0:
-                quantise_weights()

@@ -18,6 +18,7 @@ DIM = 512
 PACK = 4
 SLOTS = T // P
 G = 2
+ALL = tuple(range(G))
 UNITS = G * H
 BANK_UNITS = 3
 CTX_PAD = 8
@@ -148,59 +149,60 @@ def tile_linearattention_pb_kernel(tc, q, k_sum, context, Wp, bp, out):
                 nc.vector.reciprocal(out=d_inv[:, first : min(first + BANK_UNITS, UNITS)], in_=den)
             live[("d_inv", r)] = d_inv
 
-        def normalise(r):
+        def normalise(r, gs=ALL):
             d_inv = live[("d_inv", r)]
-            om = work.tile([P, G, 2, H, D // PACK, 2], BF16)
-            for g in range(G):
+            om = work.tile([P, len(gs), 2, H, D // PACK, 2], BF16)
+            for n, g in enumerate(gs):
                 for h in range(H):
-                    q_pairs = queries(r, g, h).rearrange("p (a u i) -> p u a i", u=2, i=2)
                     unit = g * H + h
+                    q_pairs = queries(r, g, h).rearrange("p (a u i) -> p u a i", u=2, i=2)
                     attn = live[("attn", r, unit)].rearrange("p (a u i) -> p u a i", u=2, i=2)
                     for u in range(2):
                         nc.vector.scalar_tensor_tensor(
-                            out=om[:, g, u, h, :, :],
+                            out=om[:, n, u, h, :, :],
                             in0=attn[:, u, :, :],
                             scalar=d_inv[:, unit : unit + 1],
                             in1=q_pairs[:, u, :, :],
                             op0=MULT,
                             op1=ADD,
                         )
-            live[("om", r)] = om
+            live[("om", r, gs)] = om
 
-        def transpose_outputs(r):
-            om = live[("om", r)]
-            o_bank = psum.tile([P, G, 2, P], F32, tag="o_bank")
-            for g in range(G):
+        def transpose_outputs(r, gs=ALL, bank="o_bank"):
+            om = live[("om", r, gs)]
+            o_bank = psum.tile([P, len(gs), 2, P], F32, tag=bank, name="o_bank")
+            for n in range(len(gs)):
                 for u in range(2):
-                    words = om[:, g, u].rearrange("p h a i -> p (h a i)").bitcast(F32)
-                    nc.tensor.transpose(o_bank[:, g, u, :], words, ident_words[:])
-            live[("o_bank", r)] = o_bank
+                    words = om[:, n, u].rearrange("p h a i -> p (h a i)").bitcast(F32)
+                    nc.tensor.transpose(o_bank[:, n, u, :], words, ident_words[:])
+            live[("o_bank", r, gs)] = o_bank
 
-        def regroup_outputs(r):
-            o_bank = live[("o_bank", r)]
-            grouped = work.tile([P, G, P, PACK], BF16, align_bytes=64)
-            nc.scalar.copy(out=grouped[:].bitcast(F32), in_=o_bank[:].rearrange("p g u t -> p g t u"))
-            live[("grouped", r)] = grouped
+        def regroup_outputs(r, gs=ALL):
+            grouped = work.tile([P, len(gs), P, PACK], BF16, align_bytes=64)
+            nc.scalar.copy(
+                out=grouped[:].bitcast(F32), in_=live[("o_bank", r, gs)][:].rearrange("p g u t -> p g t u")
+            )
+            live[("grouped", r, gs)] = grouped
 
-        def quantise(r):
-            codes = work.tile([P, G * P], U32, align_bytes=64)
-            scales = work.tile([P, G * P], U8, align_bytes=64)
+        def quantise(r, gs=ALL):
+            codes = work.tile([P, len(gs) * P], U32, align_bytes=64)
+            scales = work.tile([P, len(gs) * P], U8, align_bytes=64)
             nc.vector.quantize_mx(
                 out=codes[:].bitcast(FP8X4),
                 scales=scales[:],
-                in_=live[("grouped", r)][:].rearrange("p g t k -> p (g t k)"),
+                in_=live[("grouped", r, gs)][:].rearrange("p g t k -> p (g t k)"),
             )
-            live[("codes", r)] = codes
-            live[("scales", r)] = scales
+            for n, g in enumerate(gs):
+                live[("codes", r, g)] = codes[:, n * P : (n + 1) * P]
+                live[("scales", r, g)] = scales[:, n * P : (n + 1) * P]
 
-        def project(r):
-            for g in range(G):
-                tokens = slice(g * P, (g + 1) * P)
+        def project(r, gs=ALL):
+            for g in gs:
                 out_bank = psum.tile([P, DIM], F32, tag="out_bank_%d" % g, name="out_bank")
                 nc.tensor.matmul_mx(
                     out=out_bank[:],
-                    lhsT=live[("codes", r)][:, tokens].bitcast(FP8X4),
-                    lhsT_scale=live[("scales", r)][:, tokens],
+                    lhsT=live[("codes", r, g)].bitcast(FP8X4),
+                    lhsT_scale=live[("scales", r, g)],
                     rhs=w_codes[:].bitcast(FP8X4),
                     rhs_scale=w_scales[:],
                     start=True,
@@ -208,18 +210,19 @@ def tile_linearattention_pb_kernel(tc, q, k_sum, context, Wp, bp, out):
                 )
                 live[("out", r, g)] = out_bank
 
-        def add_bias_and_store(r):
+        def add_bias_and_store(r, gs=ALL):
             b, pair = divmod(r, ROUNDS_PER_BATCH)
-            result = results.tile([P, G, DIM], F32)
-            for g in range(G):
-                if (g == 1 or r % 2 == 1) and r < ROUNDS - 2:
+            result = results.tile([P, len(gs), DIM], F32)
+            for n, g in enumerate(gs):
+                if g == 1 and r < ROUNDS - 2:
                     plain = results.tile([P, DIM], F32)
                     nc.scalar.copy(out=plain[:], in_=live[("out", r, g)][:])
-                    nc.gpsimd.tensor_tensor(out=result[:, g, :], in0=plain[:], in1=bias[:], op=ADD)
+                    nc.gpsimd.tensor_tensor(out=result[:, n, :], in0=plain[:], in1=bias[:], op=ADD)
                 else:
-                    nc.vector.tensor_tensor(out=result[:, g, :], in0=live[("out", r, g)][:], in1=bias[:], op=ADD)
+                    nc.vector.tensor_tensor(out=result[:, n, :], in0=live[("out", r, g)][:], in1=bias[:], op=ADD)
             out_view = out[b].rearrange("(p j) n -> p j n", j=SLOTS)
-            nc.sync.dma_start(out=out_view[:, pair * G : (pair + 1) * G, :], in_=result[:])
+            first = pair * G + gs[0]
+            nc.sync.dma_start(out=out_view[:, first : first + len(gs), :], in_=result[:])
 
         def active(r):
             return 0 <= r < ROUNDS
@@ -230,7 +233,7 @@ def tile_linearattention_pb_kernel(tc, q, k_sum, context, Wp, bp, out):
         invert(0)
         transpose_queries(1)
         multiply_context(1)
-        for c in range(ROUNDS + 2):
+        for c in range(ROUNDS - 1):
             if c > 0 and active(c + 1):
                 transpose_queries(c + 1)
             if c == 1:
@@ -251,3 +254,25 @@ def tile_linearattention_pb_kernel(tc, q, k_sum, context, Wp, bp, out):
                 multiply_context(c + 1)
             if active(c + 1):
                 invert(c + 1)
+
+        last = ROUNDS - 1
+        transpose_outputs(last - 1)
+        regroup_outputs(last - 1)
+        quantise(last - 2)
+        project(last - 2)
+        normalise(last, (0,))
+        transpose_outputs(last, (0,))
+        quantise(last - 1)
+        normalise(last, (1,))
+        add_bias_and_store(last - 2)
+        project(last - 1)
+        transpose_outputs(last, (1,), bank="q_bank")
+        regroup_outputs(last, (0,))
+        regroup_outputs(last, (1,))
+        add_bias_and_store(last - 1, (0,))
+        quantise(last, (0,))
+        add_bias_and_store(last - 1, (1,))
+        quantise(last, (1,))
+        for g in ALL:
+            project(last, (g,))
+            add_bias_and_store(last, (g,))

@@ -151,30 +151,27 @@ def tile_linearattention_pb_kernel(tc, q, k_sum, context, Wp, bp, out):
 
         def normalise(r, gs=ALL):
             d_inv = live[("d_inv", r)]
-            om = work.tile([P, len(gs), 2, H, D // PACK, 2], BF16)
+            om = work.tile([P, len(gs), E], BF16)
             for n, g in enumerate(gs):
                 for h in range(H):
                     unit = g * H + h
-                    q_pairs = queries(r, g, h).rearrange("p (a u i) -> p u a i", u=2, i=2)
-                    attn = live[("attn", r, unit)].rearrange("p (a u i) -> p u a i", u=2, i=2)
-                    for u in range(2):
-                        nc.vector.scalar_tensor_tensor(
-                            out=om[:, n, u, h, :, :],
-                            in0=attn[:, u, :, :],
-                            scalar=d_inv[:, unit : unit + 1],
-                            in1=q_pairs[:, u, :, :],
-                            op0=MULT,
-                            op1=ADD,
-                        )
+                    nc.vector.scalar_tensor_tensor(
+                        out=om[:, n, h * D : (h + 1) * D],
+                        in0=live[("attn", r, unit)],
+                        scalar=d_inv[:, unit : unit + 1],
+                        in1=queries(r, g, h),
+                        op0=MULT,
+                        op1=ADD,
+                    )
             live[("om", r, gs)] = om
 
         def transpose_outputs(r, gs=ALL, bank="o_bank"):
             om = live[("om", r, gs)]
             o_bank = psum.tile([P, len(gs), 2, P], F32, tag=bank, name="o_bank")
             for n in range(len(gs)):
+                words = om[:, n, :].bitcast(F32)
                 for u in range(2):
-                    words = om[:, n, u].rearrange("p h a i -> p (h a i)").bitcast(F32)
-                    nc.tensor.transpose(o_bank[:, n, u, :], words, ident_words[:])
+                    nc.tensor.transpose(o_bank[:, n, u, :], words[:, u::2], ident_words[:])
             live[("o_bank", r, gs)] = o_bank
 
         def regroup_outputs(r, gs=ALL):
@@ -224,11 +221,21 @@ def tile_linearattention_pb_kernel(tc, q, k_sum, context, Wp, bp, out):
             first = pair * G + gs[0]
             nc.sync.dma_start(out=out_view[:, first : first + len(gs), :], in_=result[:])
 
+        zeros = const.tile([P, DIM], BF16)
+        nc.vector.memset(zeros[:], 0.0)
+
+        def warm_up(count):
+            zero_bank = psum.tile([P, DIM], F32, tag="q_bank", name="zero_bank")
+            for i in range(count):
+                nc.tensor.matmul(zero_bank[:], lhsT=zeros[:, 0:P], rhs=zeros[:], start=True, stop=True)
+
         def active(r):
             return 0 <= r < ROUNDS
 
+        warm_up(5)
         transpose_queries(0)
         transpose_ksum()
+        warm_up(1)
         multiply_context(0)
         invert(0)
         transpose_queries(1)

@@ -122,7 +122,8 @@ def tile_linearattention_pb_kernel(tc, q, k_sum, context, Wp, bp, out):
                 for g in range(tiles):
                     for h in range(H):
                         nc.tensor.transpose(q_bank[:, g * H + h, :], queries(r, i * tiles + g, h), ident[:])
-                nc.scalar.copy(out=q_t[:, i * tiles * H : (i + 1) * tiles * H, :], in_=q_bank[:])
+                units = slice(i * tiles * H, (i + 1) * tiles * H)
+                nc.scalar.copy(out=q_t[:, units, :].bitcast(F32), in_=q_bank[:].bitcast(F32))
             live[("q_t", r)] = q_t
 
         def multiply_context(r):

@@ -33,7 +33,7 @@ def tile_linearattention_pb_kernel(tc, q, k_sum, context, Wp, bp, out):
     with ExitStack() as stack:
         const = stack.enter_context(tc.tile_pool(name="const", bufs=1))
         work = stack.enter_context(tc.tile_pool(name="work", bufs=2))
-        results = stack.enter_context(tc.tile_pool(name="results", bufs=4))
+        results = stack.enter_context(tc.tile_pool(name="results", bufs=8))
         psum = stack.enter_context(tc.psum_pool(name="psum", bufs=1))
         stack.enter_context(tc.manual_schedule())
 
@@ -76,27 +76,31 @@ def tile_linearattention_pb_kernel(tc, q, k_sum, context, Wp, bp, out):
             nc.tensor.transpose(ksum_bank[:], ksum_rows[:], ident[:])
             nc.vector.tensor_copy(out=ctx[:, :, D], in_=ksum_bank[:, 0 : B * H])
 
+        live = {}
+
         w_codes = const.tile([P, DIM], U32, align_bytes=64)
         w_scales = const.tile([P, DIM], U8, align_bytes=64)
 
         w_grouped = const.tile([P, DIM, PACK], BF16, align_bytes=64)
 
+        w_blocks = DIM // P // G
+
         def transpose_weights():
-            w_words = w_grouped[:].bitcast(F32)
-            blocks_per_bank = DIM // P // G
             for g in range(G):
-                first = g * blocks_per_bank
-                w_bank = psum.tile([P, blocks_per_bank, 2, P], F32, tag="out_bank_%d" % g, name="w_bank")
-                for c in range(blocks_per_bank):
-                    nat_words = w_nat[:, first + c, :].bitcast(F32)
+                w_bank = psum.tile([P, w_blocks, 2, P], F32, tag="out_bank_%d" % g, name="w_bank")
+                for c in range(w_blocks):
+                    nat_words = w_nat[:, g * w_blocks + c, :].bitcast(F32)
                     for u in range(2):
                         nc.tensor.transpose(w_bank[:, c, u, :], nat_words[:, u::2], ident_words[:])
-                nc.scalar.copy(
-                    out=w_words[:, first * P : (first + blocks_per_bank) * P, :].rearrange(
-                        "p (c n) u -> p c n u", c=blocks_per_bank
-                    ),
-                    in_=w_bank[:].rearrange("p c u n -> p c n u"),
-                )
+                live[("w_bank", g)] = w_bank
+
+        def gather_weights(g, copy):
+            features = slice(g * w_blocks * P, (g + 1) * w_blocks * P)
+            w_words = w_grouped[:].bitcast(F32)[:, features, :]
+            copy(
+                out=w_words.rearrange("p (c n) u -> p c n u", c=w_blocks),
+                in_=live[("w_bank", g)][:].rearrange("p c u n -> p c n u"),
+            )
 
         def quantise_weights():
             nc.vector.quantize_mx(
@@ -105,7 +109,6 @@ def tile_linearattention_pb_kernel(tc, q, k_sum, context, Wp, bp, out):
                 in_=w_grouped[:].rearrange("p n k -> p (n k)"),
             )
 
-        live = {}
 
         def queries(r, g, h):
             b, pair = divmod(r, ROUNDS_PER_BATCH)
@@ -233,7 +236,7 @@ def tile_linearattention_pb_kernel(tc, q, k_sum, context, Wp, bp, out):
         def active(r):
             return 0 <= r < ROUNDS
 
-        warm_up(5)
+        warm_up(3)
         transpose_queries(0)
         transpose_ksum()
         warm_up(1)
@@ -246,6 +249,7 @@ def tile_linearattention_pb_kernel(tc, q, k_sum, context, Wp, bp, out):
                 transpose_queries(c + 1)
             if c == 1:
                 transpose_weights()
+                gather_weights(0, nc.scalar.copy)
             if active(c - 1):
                 transpose_outputs(c - 1)
                 regroup_outputs(c - 1)
@@ -255,6 +259,7 @@ def tile_linearattention_pb_kernel(tc, q, k_sum, context, Wp, bp, out):
             if active(c):
                 normalise(c)
             if c == 1:
+                gather_weights(1, nc.vector.tensor_copy)
                 quantise_weights()
             if active(c - 2):
                 add_bias_and_store(c - 2)
@@ -271,8 +276,8 @@ def tile_linearattention_pb_kernel(tc, q, k_sum, context, Wp, bp, out):
         normalise(last, (0,))
         transpose_outputs(last, (0,))
         quantise(last - 1)
-        normalise(last, (1,))
         add_bias_and_store(last - 2)
+        normalise(last, (1,))
         project(last - 1)
         transpose_outputs(last, (1,), bank="q_bank")
         regroup_outputs(last, (0,))

@@ -125,8 +125,12 @@ def tile_linearattention_pb_kernel(tc, q, k_sum, context, Wp, bp, out):
                 for g in range(tiles):
                     for h in range(H):
                         nc.tensor.transpose(q_bank[:, g * H + h, :], queries(r, i * tiles + g, h), ident[:])
-                units = slice(i * tiles * H, (i + 1) * tiles * H)
-                nc.scalar.copy(out=q_t[:, units, :].bitcast(F32), in_=q_bank[:].bitcast(F32))
+                for g in range(tiles):
+                    first = (i * tiles + g) * H
+                    nc.scalar.copy(
+                        out=q_t[:, first : first + H, :].bitcast(F32),
+                        in_=q_bank[:, g * H : (g + 1) * H, :].bitcast(F32),
+                    )
             live[("q_t", r)] = q_t
 
         def multiply_context(r):
@@ -225,21 +229,21 @@ def tile_linearattention_pb_kernel(tc, q, k_sum, context, Wp, bp, out):
             first = pair * G + gs[0]
             nc.sync.dma_start(out=out_view[:, first : first + len(gs), :], in_=result[:])
 
-        zeros = const.tile([P, DIM], BF16)
+        zeros = const.tile([P, 2 * P], BF16)
         nc.vector.memset(zeros[:], 0.0)
 
         def warm_up(count):
-            zero_bank = psum.tile([P, DIM], F32, tag="q_bank", name="zero_bank")
+            zero_bank = psum.tile([P, 2 * P], F32, tag="q_bank", name="zero_bank")
             for i in range(count):
                 nc.tensor.matmul(zero_bank[:], lhsT=zeros[:, 0:P], rhs=zeros[:], start=True, stop=True)
 
         def active(r):
             return 0 <= r < ROUNDS
 
-        warm_up(3)
+        warm_up(8)
         transpose_queries(0)
         transpose_ksum()
-        warm_up(1)
+        warm_up(2)
         multiply_context(0)
         invert(0)
         transpose_queries(1)

@@ -159,27 +159,30 @@ def tile_linearattention_pb_kernel(tc, q, k_sum, context, Wp, bp, out):
 
         def normalise(r, gs=ALL):
             d_inv = live[("d_inv", r)]
-            om = work.tile([P, len(gs), E], BF16)
+            om = work.tile([P, len(gs), 2, H, D // PACK, 2], BF16)
             for n, g in enumerate(gs):
                 for h in range(H):
                     unit = g * H + h
-                    nc.vector.scalar_tensor_tensor(
-                        out=om[:, n, h * D : (h + 1) * D],
-                        in0=live[("attn", r, unit)],
-                        scalar=d_inv[:, unit : unit + 1],
-                        in1=queries(r, g, h),
-                        op0=MULT,
-                        op1=ADD,
-                    )
+                    q_pairs = queries(r, g, h).rearrange("p (a u i) -> p u a i", u=2, i=2)
+                    attn = live[("attn", r, unit)].rearrange("p (a u i) -> p u a i", u=2, i=2)
+                    for u in range(2):
+                        nc.vector.scalar_tensor_tensor(
+                            out=om[:, n, u, h, :, :],
+                            in0=attn[:, u, :, :],
+                            scalar=d_inv[:, unit : unit + 1],
+                            in1=q_pairs[:, u, :, :],
+                            op0=MULT,
+                            op1=ADD,
+                        )
             live[("om", r, gs)] = om
 
         def transpose_outputs(r, gs=ALL, bank="o_bank"):
             om = live[("om", r, gs)]
             o_bank = psum.tile([P, len(gs), 2, P], F32, tag=bank, name="o_bank")
             for n in range(len(gs)):
-                words = om[:, n, :].bitcast(F32)
                 for u in range(2):
-                    nc.tensor.transpose(o_bank[:, n, u, :], words[:, u::2], ident_words[:])
+                    words = om[:, n, u].rearrange("p h a i -> p (h a i)").bitcast(F32)
+                    nc.tensor.transpose(o_bank[:, n, u, :], words, ident_words[:])
             live[("o_bank", r, gs)] = o_bank
 
         def regroup_outputs(r, gs=ALL):

from contextlib import ExitStack

import concourse.mybir as mybir
from concourse.masks import make_identity

BF16 = mybir.dt.bfloat16
F32 = mybir.dt.float32
U32 = mybir.dt.uint32
U8 = mybir.dt.uint8
FP8X4 = mybir.dt.float8_e4m3fn_x4
MULT = mybir.AluOpType.mult
ADD = mybir.AluOpType.add

P = 128
B, H, T, D = 4, 4, 1024, 128
E = H * D
DIM = 512
PACK = 4
SLOTS = T // P
G = 2
ALL = tuple(range(G))
UNITS = G * H
BANK_UNITS = 3
CTX_PAD = 8
ROUNDS_PER_BATCH = SLOTS // G
ROUNDS = B * ROUNDS_PER_BATCH

FLOPS = 2 * B * H * T * D * D + 2 * B * H * T * D + 2 * B * T * E * DIM


def tile_linearattention_pb_kernel(tc, q, k_sum, context, Wp, bp, out):
    nc = tc.nc
    with ExitStack() as stack:
        const = stack.enter_context(tc.tile_pool(name="const", bufs=1))
        work = stack.enter_context(tc.tile_pool(name="work", bufs=2))
        results = stack.enter_context(tc.tile_pool(name="results", bufs=8))
        psum = stack.enter_context(tc.psum_pool(name="psum", bufs=1))
        stack.enter_context(tc.manual_schedule())

        ident = const.tile([P, P], BF16)
        make_identity(nc, ident[:])
        ident_words = const.tile([P, P], F32)
        make_identity(nc, ident_words[:])

        ksum_rows = const.tile([P, D], BF16)
        nc.vector.memset(ksum_rows[:], 0.0)

        q_nat = {}
        ctx = const.tile([P, B * H, D + CTX_PAD], BF16)
        w_nat = const.tile([P, DIM // P, E], BF16)
        bias = const.tile([P, DIM], BF16)

        def load_queries(b, first, width):
            chunk = const.tile([P, H, width, D], BF16, name="q_nat_%d_%d" % (b, first))
            q_view = q[b].rearrange("h (p j) d -> p h j d", j=SLOTS)
            nc.sync.dma_start(out=chunk[:], in_=q_view[:, :, first : first + width, :])
            for j in range(width):
                q_nat[(b, first + j)] = (chunk, j)

        def load_context(b):
            nc.sync.dma_start(out=ctx[:, b * H : (b + 1) * H, 0:D], in_=context[b].rearrange("h d e -> d h e"))

        load_queries(0, 0, G)
        nc.sync.dma_start(out=ksum_rows[0 : B * H, :], in_=k_sum.rearrange("b h o d -> (b h o) d"))
        load_context(0)
        load_queries(0, G, G)
        nc.sync.dma_start(out=w_nat[:], in_=Wp.rearrange("(c p) k -> p c k", p=P))
        load_queries(0, 2 * G, SLOTS - 2 * G)
        nc.sync.dma_start(out=bias[:], in_=bp.partition_broadcast(P))
        for b in range(1, B):
            load_queries(b, 0, SLOTS)
            load_context(b)

        def transpose_ksum():
            ksum_bank = psum.tile([P, P], BF16, tag="o_bank")
            nc.tensor.transpose(ksum_bank[:], ksum_rows[:], ident[:])
            nc.vector.tensor_copy(out=ctx[:, :, D], in_=ksum_bank[:, 0 : B * H])

        live = {}

        w_codes = const.tile([P, DIM], U32, align_bytes=64)
        w_scales = const.tile([P, DIM], U8, align_bytes=64)

        w_grouped = const.tile([P, DIM, PACK], BF16, align_bytes=64)

        w_blocks = DIM // P // G

        def transpose_weights():
            for g in range(G):
                w_bank = psum.tile([P, w_blocks, 2, P], F32, tag="out_bank_%d" % g, name="w_bank")
                for c in range(w_blocks):
                    nat_words = w_nat[:, g * w_blocks + c, :].bitcast(F32)
                    for u in range(2):
                        nc.tensor.transpose(w_bank[:, c, u, :], nat_words[:, u::2], ident_words[:])
                live[("w_bank", g)] = w_bank

        def gather_weights(g, copy):
            features = slice(g * w_blocks * P, (g + 1) * w_blocks * P)
            w_words = w_grouped[:].bitcast(F32)[:, features, :]
            copy(
                out=w_words.rearrange("p (c n) u -> p c n u", c=w_blocks),
                in_=live[("w_bank", g)][:].rearrange("p c u n -> p c n u"),
            )

        def quantise_weights():
            nc.vector.quantize_mx(
                out=w_codes[:].bitcast(FP8X4),
                scales=w_scales[:],
                in_=w_grouped[:].rearrange("p n k -> p (n k)"),
            )


        def queries(r, g, h):
            b, pair = divmod(r, ROUNDS_PER_BATCH)
            chunk, j = q_nat[(b, pair * G + g)]
            return chunk[:, h, j, :]

        def transpose_queries(r):
            q_t = work.tile([P, UNITS, P], BF16)
            early_banks = {0: ["out_bank_0", "out_bank_1"], 1: ["q_bank", "o_bank"]}
            banks = early_banks.get(r, ["q_bank"])
            tiles = G // len(banks)
            for i in range(len(banks)):
                q_bank = psum.tile([P, tiles * H, P], BF16, tag=banks[i], name="q_bank")
                for g in range(tiles):
                    for h in range(H):
                        nc.tensor.transpose(q_bank[:, g * H + h, :], queries(r, i * tiles + g, h), ident[:])
                for g in range(tiles):
                    first = (i * tiles + g) * H
                    nc.scalar.copy(
                        out=q_t[:, first : first + H, :].bitcast(F32),
                        in_=q_bank[:, g * H : (g + 1) * H, :].bitcast(F32),
                    )
            live[("q_t", r)] = q_t

        def multiply_context(r):
            b = r // ROUNDS_PER_BATCH
            q_t = live[("q_t", r)]
            for first in range(0, UNITS, BANK_UNITS):
                units = range(first, min(first + BANK_UNITS, UNITS))
                attn_bank = psum.tile([P, BANK_UNITS, D + 1], F32, bufs=4)
                for u in units:
                    nc.tensor.matmul(
                        attn_bank[:, u - first, :],
                        lhsT=q_t[:, u, :],
                        rhs=ctx[:, b * H + u % H, 0 : D + 1],
                        start=True,
                        stop=True,
                    )
                    live[("attn", r, u)] = attn_bank[:, u - first, 0:D]
                live[("den", r, first)] = attn_bank[:, 0 : len(units), D]

        def invert(r):
            d_inv = work.tile([P, UNITS], F32)
            for first in range(0, UNITS, BANK_UNITS):
                den = live[("den", r, first)]
                nc.vector.reciprocal(out=d_inv[:, first : min(first + BANK_UNITS, UNITS)], in_=den)
            live[("d_inv", r)] = d_inv

        def normalise(r, gs=ALL):
            d_inv = live[("d_inv", r)]
            om = work.tile([P, len(gs), 2, H, D // PACK, 2], BF16)
            for n, g in enumerate(gs):
                for h in range(H):
                    unit = g * H + h
                    q_pairs = queries(r, g, h).rearrange("p (a u i) -> p u a i", u=2, i=2)
                    attn = live[("attn", r, unit)].rearrange("p (a u i) -> p u a i", u=2, i=2)
                    for u in range(2):
                        nc.vector.scalar_tensor_tensor(
                            out=om[:, n, u, h, :, :],
                            in0=attn[:, u, :, :],
                            scalar=d_inv[:, unit : unit + 1],
                            in1=q_pairs[:, u, :, :],
                            op0=MULT,
                            op1=ADD,
                        )
            live[("om", r, gs)] = om

        def transpose_outputs(r, gs=ALL, bank="o_bank"):
            om = live[("om", r, gs)]
            o_bank = psum.tile([P, len(gs), 2, P], F32, tag=bank, name="o_bank")
            for n in range(len(gs)):
                for u in range(2):
                    words = om[:, n, u].rearrange("p h a i -> p (h a i)").bitcast(F32)
                    nc.tensor.transpose(o_bank[:, n, u, :], words, ident_words[:])
            live[("o_bank", r, gs)] = o_bank

        def regroup_outputs(r, gs=ALL):
            grouped = work.tile([P, len(gs), P, PACK], BF16, align_bytes=64)
            nc.scalar.copy(
                out=grouped[:].bitcast(F32), in_=live[("o_bank", r, gs)][:].rearrange("p g u t -> p g t u")
            )
            live[("grouped", r, gs)] = grouped

        def quantise(r, gs=ALL):
            codes = work.tile([P, len(gs) * P], U32, align_bytes=64)
            scales = work.tile([P, len(gs) * P], U8, align_bytes=64)
            nc.vector.quantize_mx(
                out=codes[:].bitcast(FP8X4),
                scales=scales[:],
                in_=live[("grouped", r, gs)][:].rearrange("p g t k -> p (g t k)"),
            )
            for n, g in enumerate(gs):
                live[("codes", r, g)] = codes[:, n * P : (n + 1) * P]
                live[("scales", r, g)] = scales[:, n * P : (n + 1) * P]

        def project(r, gs=ALL):
            for g in gs:
                out_bank = psum.tile([P, DIM], F32, tag="out_bank_%d" % g, name="out_bank")
                nc.tensor.matmul_mx(
                    out=out_bank[:],
                    lhsT=live[("codes", r, g)].bitcast(FP8X4),
                    lhsT_scale=live[("scales", r, g)],
                    rhs=w_codes[:].bitcast(FP8X4),
                    rhs_scale=w_scales[:],
                    start=True,
                    stop=True,
                )
                live[("out", r, g)] = out_bank

        def add_bias_and_store(r, gs=ALL):
            b, pair = divmod(r, ROUNDS_PER_BATCH)
            result = results.tile([P, len(gs), DIM], F32)
            for n, g in enumerate(gs):
                if g == 1 and r < ROUNDS - 2:
                    plain = results.tile([P, DIM], F32)
                    nc.scalar.copy(out=plain[:], in_=live[("out", r, g)][:])
                    nc.gpsimd.tensor_tensor(out=result[:, n, :], in0=plain[:], in1=bias[:], op=ADD)
                else:
                    nc.vector.tensor_tensor(out=result[:, n, :], in0=live[("out", r, g)][:], in1=bias[:], op=ADD)
            out_view = out[b].rearrange("(p j) n -> p j n", j=SLOTS)
            first = pair * G + gs[0]
            nc.sync.dma_start(out=out_view[:, first : first + len(gs), :], in_=result[:])

        zeros = const.tile([P, 2 * P], BF16)
        nc.vector.memset(zeros[:], 0.0)

        def warm_up(count):
            zero_bank = psum.tile([P, 2 * P], F32, tag="q_bank", name="zero_bank")
            for i in range(count):
                nc.tensor.matmul(zero_bank[:], lhsT=zeros[:, 0:P], rhs=zeros[:], start=True, stop=True)

        def active(r):
            return 0 <= r < ROUNDS

        warm_up(8)
        transpose_queries(0)
        transpose_ksum()
        warm_up(2)
        multiply_context(0)
        invert(0)
        transpose_queries(1)
        multiply_context(1)
        for c in range(ROUNDS - 1):
            if c > 0 and active(c + 1):
                transpose_queries(c + 1)
            if c == 1:
                transpose_weights()
                gather_weights(0, nc.scalar.copy)
            if active(c - 1):
                transpose_outputs(c - 1)
                regroup_outputs(c - 1)
            if active(c - 2):
                quantise(c - 2)
                project(c - 2)
            if active(c):
                normalise(c)
            if c == 1:
                gather_weights(1, nc.vector.tensor_copy)
                quantise_weights()
            if active(c - 2):
                add_bias_and_store(c - 2)
            if c > 0 and active(c + 1):
                multiply_context(c + 1)
            if active(c + 1):
                invert(c + 1)

        last = ROUNDS - 1
        transpose_outputs(last - 1)
        regroup_outputs(last - 1)
        quantise(last - 2)
        project(last - 2)
        normalise(last, (0,))
        transpose_outputs(last, (0,))
        quantise(last - 1)
        add_bias_and_store(last - 2)
        normalise(last, (1,))
        project(last - 1)
        transpose_outputs(last, (1,), bank="q_bank")
        regroup_outputs(last, (0,))
        regroup_outputs(last, (1,))
        add_bias_and_store(last - 1, (0,))
        quantise(last, (0,))
        add_bias_and_store(last - 1, (1,))
        quantise(last, (1,))
        for g in ALL:
            project(last, (g,))
            add_bias_and_store(last, (g,))
